import numpy as np
import ml_dtypes

BF16 = ml_dtypes.bfloat16


def bf(x):
    return np.asarray(x, np.float32).astype(BF16)


def f32(x):
    return np.asarray(x, np.float32)


def f64(x):
    return np.asarray(x).astype(np.float64)


def striped(idx):
    return np.tile(idx.reshape(-1, 16).T, (8, 1))


B, H, S, N, C = 2, 128, 256, 512, 256


def setup_inputs():
    return {"p_log": f32(np.random.uniform(size=(C, S))), "p_first": bf(np.random.uniform(size=(C, N))), "d_error": bf(np.random.uniform(size=(H, H)) * (8.0 / H)), "offs": striped(np.random.permutation(np.tile(np.arange(S), 2))[:N])}


def reference(p_log, p_first, d_error, offs):
    idx = offs[:16].T.reshape(-1)
    t = np.einsum("hk,bhn->bkn", f64(d_error), f64(p_first).reshape(B, H, N)).reshape(C, N)
    return f64(p_log)[:, idx] * t

@@ -1,0 +1,46 @@
+import concourse.mybir as mybir
+
+SAMPLES = 2
+QUBITS = 128
+LOGICAL = 256
+EDGES = 512
+PIECE = 256
+PIECE_COLS = PIECE // 16
+
+F32, BF16, U16 = mybir.dt.float32, mybir.dt.bfloat16, mybir.dt.uint16
+FLOPS = 2 * SAMPLES * QUBITS * QUBITS * EDGES
+
+
+def tile_stage2loss_kernel(tc, p_log, p_first, d_error, offs, out):
+    nc = tc.nc
+    mult = mybir.AluOpType.mult
+    with (
+        tc.tile_pool(name="held", bufs=1) as held,
+        tc.psum_pool(name="psum", bufs=1) as psum,
+    ):
+        offsets = held.tile([128, EDGES // 16], U16, name="offsets")
+        nc.sync.dma_start(offsets[:], offs)
+        distance = held.tile([QUBITS, QUBITS], BF16, name="distance")
+        nc.scalar.dma_start(distance[:], d_error)
+
+        blocks = [slice(b * QUBITS, (b + 1) * QUBITS) for b in range(SAMPLES)]
+        firsts = [held.tile([QUBITS, EDGES], BF16, name=f"first{b}") for b in range(SAMPLES)]
+        windows = [held.tile([QUBITS, LOGICAL], F32, name=f"window{b}") for b in range(SAMPLES)]
+        for b in range(SAMPLES):
+            nc.scalar.dma_start(firsts[b][:], p_first[blocks[b], :])
+            nc.sync.dma_start(windows[b][:], p_log[blocks[b], :])
+
+        for b in range(SAMPLES):
+            carried = psum.tile([QUBITS, EDGES], F32, name=f"carried{b}")
+            nc.tensor.matmul(carried[:], distance[:], firsts[b][:], start=True, stop=True)
+            carried_sb = held.tile([QUBITS, EDGES], F32, name=f"carried_sb{b}")
+            nc.scalar.copy(carried_sb[:], carried[:])
+            product = held.tile([QUBITS, EDGES], F32, name=f"product{b}")
+            for piece in range(EDGES // PIECE):
+                edges = slice(piece * PIECE, (piece + 1) * PIECE)
+                picked = windows[b][:].indirect(
+                    offsets[:, piece * PIECE_COLS : (piece + 1) * PIECE_COLS]
+                )
+                nc.vector.tensor_tensor(product[:, edges], picked, carried_sb[:, edges], mult)
+                queue = nc.sync if piece % 2 == 0 else nc.scalar
+                queue.dma_start(out[blocks[b], edges], product[:, edges])

@@ -4,7 +4,8 @@ SAMPLES = 2
 QUBITS = 128
 LOGICAL = 256
 EDGES = 512
-PIECE = 256
+PIECE = 128
+PIECES = EDGES // PIECE
 PIECE_COLS = PIECE // 16
 
 F32, BF16, U16 = mybir.dt.float32, mybir.dt.bfloat16, mybir.dt.uint16
@@ -19,28 +20,26 @@ def tile_stage2loss_kernel(tc, p_log, p_first, d_error, offs, out):
         tc.psum_pool(name="psum", bufs=1) as psum,
     ):
         offsets = held.tile([128, EDGES // 16], U16, name="offsets")
-        nc.sync.dma_start(offsets[:], offs)
         distance = held.tile([QUBITS, QUBITS], BF16, name="distance")
-        nc.scalar.dma_start(distance[:], d_error)
-
         blocks = [slice(b * QUBITS, (b + 1) * QUBITS) for b in range(SAMPLES)]
         firsts = [held.tile([QUBITS, EDGES], BF16, name=f"first{b}") for b in range(SAMPLES)]
         windows = [held.tile([QUBITS, LOGICAL], F32, name=f"window{b}") for b in range(SAMPLES)]
+        nc.sync.dma_start(offsets[:], offs)
+        nc.scalar.dma_start(distance[:], d_error)
         for b in range(SAMPLES):
             nc.scalar.dma_start(firsts[b][:], p_first[blocks[b], :])
             nc.sync.dma_start(windows[b][:], p_log[blocks[b], :])
 
         for b in range(SAMPLES):
-            carried = psum.tile([QUBITS, EDGES], F32, name=f"carried{b}")
-            nc.tensor.matmul(carried[:], distance[:], firsts[b][:], start=True, stop=True)
             carried_sb = held.tile([QUBITS, EDGES], F32, name=f"carried_sb{b}")
-            nc.scalar.copy(carried_sb[:], carried[:])
             product = held.tile([QUBITS, EDGES], F32, name=f"product{b}")
-            for piece in range(EDGES // PIECE):
+            for piece in range(PIECES):
                 edges = slice(piece * PIECE, (piece + 1) * PIECE)
+                carried = psum.tile([QUBITS, PIECE], F32, name=f"carried{b}_{piece}")
+                nc.tensor.matmul(carried[:], distance[:], firsts[b][:, edges], start=True, stop=True)
+                nc.scalar.copy(carried_sb[:, edges], carried[:])
                 picked = windows[b][:].indirect(
                     offsets[:, piece * PIECE_COLS : (piece + 1) * PIECE_COLS]
                 )
                 nc.vector.tensor_tensor(product[:, edges], picked, carried_sb[:, edges], mult)
-                queue = nc.sync if piece % 2 == 0 else nc.scalar
-                queue.dma_start(out[blocks[b], edges], product[:, edges])
+                nc.sync.dma_start(out[blocks[b], edges], product[:, edges])

@@ -24,11 +24,12 @@ def tile_stage2loss_kernel(tc, p_log, p_first, d_error, offs, out):
         blocks = [slice(b * QUBITS, (b + 1) * QUBITS) for b in range(SAMPLES)]
         firsts = [held.tile([QUBITS, EDGES], BF16, name=f"first{b}") for b in range(SAMPLES)]
         windows = [held.tile([QUBITS, LOGICAL], F32, name=f"window{b}") for b in range(SAMPLES)]
-        nc.sync.dma_start(offsets[:], offs)
+        nc.sync.dma_start(firsts[0][:], p_first[blocks[0], :])
         nc.scalar.dma_start(distance[:], d_error)
-        for b in range(SAMPLES):
-            nc.scalar.dma_start(firsts[b][:], p_first[blocks[b], :])
-            nc.sync.dma_start(windows[b][:], p_log[blocks[b], :])
+        nc.sync.dma_start(offsets[:], offs)
+        nc.scalar.dma_start(windows[0][:], p_log[blocks[0], :])
+        nc.sync.dma_start(firsts[1][:], p_first[blocks[1], :])
+        nc.scalar.dma_start(windows[1][:], p_log[blocks[1], :])
 
         for b in range(SAMPLES):
             carried_sb = held.tile([QUBITS, EDGES], F32, name=f"carried_sb{b}")

@@ -24,12 +24,12 @@ def tile_stage2loss_kernel(tc, p_log, p_first, d_error, offs, out):
         blocks = [slice(b * QUBITS, (b + 1) * QUBITS) for b in range(SAMPLES)]
         firsts = [held.tile([QUBITS, EDGES], BF16, name=f"first{b}") for b in range(SAMPLES)]
         windows = [held.tile([QUBITS, LOGICAL], F32, name=f"window{b}") for b in range(SAMPLES)]
+        nc.sync.dma_start(distance[:], d_error)
         nc.sync.dma_start(firsts[0][:], p_first[blocks[0], :])
-        nc.scalar.dma_start(distance[:], d_error)
         nc.sync.dma_start(offsets[:], offs)
-        nc.scalar.dma_start(windows[0][:], p_log[blocks[0], :])
+        nc.sync.dma_start(windows[0][:], p_log[blocks[0], :])
         nc.sync.dma_start(firsts[1][:], p_first[blocks[1], :])
-        nc.scalar.dma_start(windows[1][:], p_log[blocks[1], :])
+        nc.sync.dma_start(windows[1][:], p_log[blocks[1], :])
 
         for b in range(SAMPLES):
             carried_sb = held.tile([QUBITS, EDGES], F32, name=f"carried_sb{b}")

@@ -7,6 +7,7 @@ EDGES = 512
 PIECE = 128
 PIECES = EDGES // PIECE
 PIECE_COLS = PIECE // 16
+HALF = EDGES // 2
 
 F32, BF16, U16 = mybir.dt.float32, mybir.dt.bfloat16, mybir.dt.uint16
 FLOPS = 2 * SAMPLES * QUBITS * QUBITS * EDGES
@@ -25,9 +26,10 @@ def tile_stage2loss_kernel(tc, p_log, p_first, d_error, offs, out):
         firsts = [held.tile([QUBITS, EDGES], BF16, name=f"first{b}") for b in range(SAMPLES)]
         windows = [held.tile([QUBITS, LOGICAL], F32, name=f"window{b}") for b in range(SAMPLES)]
         nc.sync.dma_start(distance[:], d_error)
-        nc.sync.dma_start(firsts[0][:], p_first[blocks[0], :])
+        nc.sync.dma_start(firsts[0][:, :HALF], p_first[blocks[0], :HALF])
         nc.sync.dma_start(offsets[:], offs)
         nc.sync.dma_start(windows[0][:], p_log[blocks[0], :])
+        nc.sync.dma_start(firsts[0][:, HALF:], p_first[blocks[0], HALF:])
         nc.sync.dma_start(firsts[1][:], p_first[blocks[1], :])
         nc.sync.dma_start(windows[1][:], p_log[blocks[1], :])
 

@@ -30,8 +30,9 @@ def tile_stage2loss_kernel(tc, p_log, p_first, d_error, offs, out):
         nc.sync.dma_start(offsets[:], offs)
         nc.sync.dma_start(windows[0][:], p_log[blocks[0], :])
         nc.sync.dma_start(firsts[0][:, HALF:], p_first[blocks[0], HALF:])
-        nc.sync.dma_start(firsts[1][:], p_first[blocks[1], :])
+        nc.sync.dma_start(firsts[1][:, :HALF], p_first[blocks[1], :HALF])
         nc.sync.dma_start(windows[1][:], p_log[blocks[1], :])
+        nc.sync.dma_start(firsts[1][:, HALF:], p_first[blocks[1], HALF:])
 
         for b in range(SAMPLES):
             carried_sb = held.tile([QUBITS, EDGES], F32, name=f"carried_sb{b}")

@@ -4,10 +4,11 @@ SAMPLES = 2
 QUBITS = 128
 LOGICAL = 256
 EDGES = 512
-PIECE = 128
-PIECES = EDGES // PIECE
-PIECE_COLS = PIECE // 16
 HALF = EDGES // 2
+WIDTHS = ((64, 64, 128, 128, 128), (128, 128, 128, 128))
+assert all(sum(widths) == EDGES and max(widths) <= LOGICAL for widths in WIDTHS)
+PSUM_BANKS = 8
+STORE = 128
 
 F32, BF16, U16 = mybir.dt.float32, mybir.dt.bfloat16, mybir.dt.uint16
 FLOPS = 2 * SAMPLES * QUBITS * QUBITS * EDGES
@@ -18,7 +19,7 @@ def tile_stage2loss_kernel(tc, p_log, p_first, d_error, offs, out):
     mult = mybir.AluOpType.mult
     with (
         tc.tile_pool(name="held", bufs=1) as held,
-        tc.psum_pool(name="psum", bufs=1) as psum,
+        tc.psum_pool(name="psum", bufs=PSUM_BANKS) as psum,
     ):
         offsets = held.tile([128, EDGES // 16], U16, name="offsets")
         distance = held.tile([QUBITS, QUBITS], BF16, name="distance")
@@ -37,13 +38,16 @@ def tile_stage2loss_kernel(tc, p_log, p_first, d_error, offs, out):
         for b in range(SAMPLES):
             carried_sb = held.tile([QUBITS, EDGES], F32, name=f"carried_sb{b}")
             product = held.tile([QUBITS, EDGES], F32, name=f"product{b}")
-            for piece in range(PIECES):
-                edges = slice(piece * PIECE, (piece + 1) * PIECE)
-                carried = psum.tile([QUBITS, PIECE], F32, name=f"carried{b}_{piece}")
+            start = 0
+            stored = 0
+            for width in WIDTHS[b]:
+                edges = slice(start, start + width)
+                carried = psum.tile([QUBITS, width], F32, tag="carried")
                 nc.tensor.matmul(carried[:], distance[:], firsts[b][:, edges], start=True, stop=True)
                 nc.scalar.copy(carried_sb[:, edges], carried[:])
-                picked = windows[b][:].indirect(
-                    offsets[:, piece * PIECE_COLS : (piece + 1) * PIECE_COLS]
-                )
+                picked = windows[b][:].indirect(offsets[:, start // 16 : (start + width) // 16])
                 nc.vector.tensor_tensor(product[:, edges], picked, carried_sb[:, edges], mult)
-                nc.sync.dma_start(out[blocks[b], edges], product[:, edges])
+                start += width
+                if start - stored >= STORE:
+                    nc.sync.dma_start(out[blocks[b], stored:start], product[:, stored:start])
+                    stored = start

@@ -5,10 +5,9 @@ QUBITS = 128
 LOGICAL = 256
 EDGES = 512
 HALF = EDGES // 2
-WIDTHS = ((64, 64, 128, 128, 128), (128, 128, 128, 128))
+WIDTHS = ((64, 64, 128, 128, 128), (192, 192, 128))
 assert all(sum(widths) == EDGES and max(widths) <= LOGICAL for widths in WIDTHS)
 PSUM_BANKS = 8
-STORE = 128
 
 F32, BF16, U16 = mybir.dt.float32, mybir.dt.bfloat16, mybir.dt.uint16
 FLOPS = 2 * SAMPLES * QUBITS * QUBITS * EDGES
@@ -39,7 +38,6 @@ def tile_stage2loss_kernel(tc, p_log, p_first, d_error, offs, out):
             carried_sb = held.tile([QUBITS, EDGES], F32, name=f"carried_sb{b}")
             product = held.tile([QUBITS, EDGES], F32, name=f"product{b}")
             start = 0
-            stored = 0
             for width in WIDTHS[b]:
                 edges = slice(start, start + width)
                 carried = psum.tile([QUBITS, width], F32, tag="carried")
@@ -47,7 +45,5 @@ def tile_stage2loss_kernel(tc, p_log, p_first, d_error, offs, out):
                 nc.scalar.copy(carried_sb[:, edges], carried[:])
                 picked = windows[b][:].indirect(offsets[:, start // 16 : (start + width) // 16])
                 nc.vector.tensor_tensor(product[:, edges], picked, carried_sb[:, edges], mult)
+                nc.sync.dma_start(out[blocks[b], edges], product[:, edges])
                 start += width
-                if start - stored >= STORE:
-                    nc.sync.dma_start(out[blocks[b], stored:start], product[:, stored:start])
-                    stored = start

import concourse.mybir as mybir

SAMPLES = 2
QUBITS = 128
LOGICAL = 256
EDGES = 512
HALF = EDGES // 2
WIDTHS = ((64, 64, 128, 128, 128), (192, 192, 128))
assert all(sum(widths) == EDGES and max(widths) <= LOGICAL for widths in WIDTHS)
PSUM_BANKS = 8

F32, BF16, U16 = mybir.dt.float32, mybir.dt.bfloat16, mybir.dt.uint16
FLOPS = 2 * SAMPLES * QUBITS * QUBITS * EDGES


def tile_stage2loss_kernel(tc, p_log, p_first, d_error, offs, out):
    nc = tc.nc
    mult = mybir.AluOpType.mult
    with (
        tc.tile_pool(name="held", bufs=1) as held,
        tc.psum_pool(name="psum", bufs=PSUM_BANKS) as psum,
    ):
        offsets = held.tile([128, EDGES // 16], U16, name="offsets")
        distance = held.tile([QUBITS, QUBITS], BF16, name="distance")
        blocks = [slice(b * QUBITS, (b + 1) * QUBITS) for b in range(SAMPLES)]
        firsts = [held.tile([QUBITS, EDGES], BF16, name=f"first{b}") for b in range(SAMPLES)]
        windows = [held.tile([QUBITS, LOGICAL], F32, name=f"window{b}") for b in range(SAMPLES)]
        nc.sync.dma_start(distance[:], d_error)
        nc.sync.dma_start(firsts[0][:, :HALF], p_first[blocks[0], :HALF])
        nc.sync.dma_start(offsets[:], offs)
        nc.sync.dma_start(windows[0][:], p_log[blocks[0], :])
        nc.sync.dma_start(firsts[0][:, HALF:], p_first[blocks[0], HALF:])
        nc.sync.dma_start(firsts[1][:, :HALF], p_first[blocks[1], :HALF])
        nc.sync.dma_start(windows[1][:], p_log[blocks[1], :])
        nc.sync.dma_start(firsts[1][:, HALF:], p_first[blocks[1], HALF:])

        for b in range(SAMPLES):
            carried_sb = held.tile([QUBITS, EDGES], F32, name=f"carried_sb{b}")
            product = held.tile([QUBITS, EDGES], F32, name=f"product{b}")
            start = 0
            for width in WIDTHS[b]:
                edges = slice(start, start + width)
                carried = psum.tile([QUBITS, width], F32, tag="carried")
                nc.tensor.matmul(carried[:], distance[:], firsts[b][:, edges], start=True, stop=True)
                nc.scalar.copy(carried_sb[:, edges], carried[:])
                picked = windows[b][:].indirect(offsets[:, start // 16 : (start + width) // 16])
                nc.vector.tensor_tensor(product[:, edges], picked, carried_sb[:, edges], mult)
                nc.sync.dma_start(out[blocks[b], edges], product[:, edges])
                start += width
